import numpy as np
import ml_dtypes


def mxq(x, axis, fmt="e4m3"):
    dtype, down = {"e4m3": (ml_dtypes.float8_e4m3fn, 7), "e5m2": (ml_dtypes.float8_e5m2, 14)}[fmt]
    v = np.moveaxis(np.asarray(x, np.float32).astype(ml_dtypes.bfloat16).astype(np.float64), axis, -1)
    blocks = v.reshape(v.shape[:-1] + (-1, 32))
    amax = np.abs(blocks).max(-1, keepdims=True)
    byte = np.maximum(np.where(amax > 0, np.frexp(amax)[1] - 1 + 127, 0) - down, 1)
    scale = np.exp2(byte - 127.0)
    codes = (blocks / scale).astype(np.float32).astype(dtype).astype(np.float64)
    return np.moveaxis((codes * scale).reshape(v.shape), -1, axis)


WIDE = False


def mx_kscale(k):
    if not WIDE:
        return np.ones(k)
    levels = np.array([18, -18])
    if k % 512:
        return np.exp2(np.random.permutation(np.resize(levels, k // 32))).repeat(32)
    a = np.empty((k // 512, 16))
    for p in range(k // 512):
        a[p, :8] = np.random.permutation(np.resize(levels, 8))
        for g in range(8):
            far = levels[np.abs(levels - a[p, g]) >= 10]
            a[p, g + 8] = far[np.random.randint(len(far))]
    return np.exp2(a.ravel()).repeat(32)


BF16 = ml_dtypes.bfloat16


def bf(x):
    return np.asarray(x, np.float32).astype(BF16)


def f64(x):
    return np.asarray(x).astype(np.float64)


BS, DC, R, C = 2, 1024, 32, 32
N = R * C
THRESH = 0.85


def threshold(W):
    return np.where(W > THRESH, W, 0.0)


def setup_inputs():
    s = mx_kscale(N)
    s = s / s.max()
    u = mx_kscale(DC)
    seg0 = bf(np.random.standard_normal((BS, DC, R, C)) * 0.1 * np.sqrt(N))
    a = np.random.random_sample((BS, N, N))
    W0 = f64(bf(np.where(a > THRESH, a + 0.05, a * 0.94)))
    rowsum = threshold(W0).sum(axis=-1)
    g = np.random.standard_normal((BS, DC, N)) * np.exp2(np.random.randint(-6, 1, (BS, 1, N))) * 16.0
    g = g * s[None, None, :] * u[None, :, None]
    return {"seg": bf(f64(seg0) / u[None, :, None, None]),
            "W": bf(np.where(W0 > THRESH, W0 / s[None, :, None], W0)),
            "rowsum": np.asarray(rowsum, np.float32),
            "grad_out": bf(g.reshape(BS, DC, R, C))}


def reference(seg, W, rowsum, grad_out):
    seg, W, rowsum, grad_out = f64(seg), f64(W), f64(rowsum), f64(grad_out)
    bs, d, r, c = seg.shape
    n = r * c
    seg_flat = seg.reshape(bs, d, n)
    g = grad_out.reshape(bs, d, n)
    rs = rowsum[:, :, None]
    D = threshold(W) / rs
    dseg = mxq(g, 2, "e5m2") @ mxq(D, 1, "e4m3")
    dD = mxq(g, 1, "e5m2").transpose(0, 2, 1) @ mxq(seg_flat, 1, "e4m3")
    cm = (dD * D).sum(axis=-1, keepdims=True)
    dW = np.where(W > THRESH, (dD - cm) / rs, 0.0)
    return dseg.reshape(bs, d, r, c), dW

from contextlib import ExitStack

import concourse.mybir as mybir
from concourse.masks import make_identity

BS, DC, N = 2, 1024, 1024
THRESH = 0.85
FLOPS = 2 * 2 * BS * DC * N * N

F32 = mybir.dt.float32
BF16 = mybir.dt.bfloat16
U32 = mybir.dt.uint32
U8 = mybir.dt.uint8
E4M3 = mybir.dt.float8_e4m3fn_x4
E5M2 = mybir.dt.float8_e5m2_x4
ALU = mybir.AluOpType
COPY = mybir.ActivationFunctionType.Copy

P = 128
J = 4
GROUP = P * J
HALF = 512


def tile_regu_diff_v_kernel(tc, seg, W, rowsum, grad_out, out_0, out_1):
    nc = tc.nc
    g_v = grad_out.rearrange("b (g p j) r c -> b g p j (r c)", p=P, j=J)
    seg_v = seg.rearrange("b (g p j) r c -> b g p j (r c)", p=P, j=J)
    w_v = W.rearrange("b (g p j) n -> b g p j n", p=P, j=J)
    rs_v = rowsum.rearrange("b (g p j) -> p (b g) j", p=P, j=J)
    o0_v = out_0.rearrange("b (g p j) r c -> b g j p (r c)", p=P, j=J)
    o1_v = out_1.rearrange("b (g p j) n -> b g j p n", p=P, j=J)

    with ExitStack() as ctx:
        const = ctx.enter_context(tc.tile_pool(name="const", bufs=1))
        pin = ctx.enter_context(tc.tile_pool(name="pin", bufs=2))
        pcode = ctx.enter_context(tc.tile_pool(name="pcode", bufs=4))
        pwork = ctx.enter_context(tc.tile_pool(name="pwork", bufs=2))
        pout = ctx.enter_context(tc.tile_pool(name="pout", bufs=3))
        psum = ctx.enter_context(tc.psum_pool(name="psum", bufs=1))

        g_t, s_t, w_t, mask_t, dn_t = {}, {}, {}, {}, {}
        gq, sq, tq, dq = {}, {}, {}, {}
        gi, si, ti, di = {}, {}, {}, {}

        def load_g(b, k):
            t = pin.tile([P, J, N], BF16, name="g_nat", tag="g_nat", bufs=2)
            nc.sync.dma_start(out=t[:], in_=g_v[b, k])
            g_t[b, k] = t

        def load_s(b, k):
            t = pin.tile([P, J, N], BF16, name="s_nat", tag="s_nat", bufs=2)
            nc.sync.dma_start(out=t[:], in_=seg_v[b, k])
            s_t[b, k] = t

        def load_w(b, k):
            t = pin.tile([P, J, N], BF16, name="w_nat", tag="w_nat", bufs=3)
            for h in range(2):
                nc.sync.dma_start(out=t[:, 2 * h : 2 * h + 2, :], in_=w_v[b, k, :, 2 * h : 2 * h + 2, :])
            w_t[b, k] = t

        rs = const.tile([P, 2 * BS, J], F32, name="rs")
        rinv = const.tile([P, 2 * BS, J], F32, name="rinv")
        idf = const.tile([P, P], F32, name="idf")
        idb = const.tile([P, P], BF16, name="idb")

        load_w(0, 0)
        nc.scalar.dma_start(out=rs[:], in_=rs_v)
        load_g(0, 0)
        load_g(0, 1)
        load_s(0, 0)
        load_w(0, 1)
        load_s(0, 1)
        load_w(1, 0)
        make_identity(nc, idf[:])
        make_identity(nc, idb[:])
        nc.vector.reciprocal(out=rinv[:], in_=rs[:])

        def codes(store, b, k, what):
            if (b, k) not in store:
                c = pcode.tile([P, N], U32, name="c_" + what, tag="c_" + what, bufs=4, align_bytes=64)
                s = pcode.tile([P, N], U8, name="x_" + what, tag="x_" + what, bufs=4, align_bytes=64)
                store[b, k] = (c, s)
            return store[b, k]

        def quant(store, b, k, h, what, src, fmt):
            c, s = codes(store, b, k, what)
            cols = slice(h * HALF, (h + 1) * HALF)
            nc.vector.quantize_mx(
                out=c[:, cols].bitcast(fmt), scales=s[:, cols], in_=src[:].rearrange("p w j -> p (w j)")
            )

        def wp(b, k):
            w = w_t[b, k]
            m = pin.tile([P, J, N], BF16, name="mask", tag="mask", bufs=2)
            d = pin.tile([P, J, N], BF16, name="dn", tag="dn", bufs=2)
            mask_t[b, k], dn_t[b, k] = m, d
            step = 2 if (b, k) == (0, 0) else J
            for h in range(0, J, step):
                js = slice(h, h + step)
                nc.vector.tensor_scalar(out=m[:, js, :], in0=w[:, js, :], scalar1=THRESH, scalar2=None, op0=ALU.is_gt)
                nc.vector.tensor_tensor(out=w[:, js, :], in0=w[:, js, :], in1=m[:, js, :], op=ALU.mult)
            for j in range(J):
                nc.vector.tensor_scalar(
                    out=d[:, j, :], in0=w[:, j, :], scalar1=rinv[:, 2 * b + k, j : j + 1], scalar2=None, op0=ALU.mult
                )

        def itile(name):
            return pwork.tile([P, HALF, J], BF16, name=name, tag=name, bufs=2, align_bytes=64)

        def tg(b, k, gm, eng):
            t = itile("g_int")
            gi[b, k, gm] = t
            dst = t[:].rearrange("p (t c) j -> p t c j", t=J)
            src = g_t[b, k][:, :, gm * GROUP : (gm + 1) * GROUP].rearrange("p j (c t) -> p t c j", t=J)
            if eng == "v":
                nc.vector.tensor_copy(out=dst, in_=src)
            else:
                nc.scalar.copy(out=dst, in_=src)

        def qg(b, k, gm):
            quant(gq, b, k, gm, "g", gi[b, k, gm], E5M2)

        def sg(b, k, h):
            t = itile("s_int")
            si[b, k, h] = t
            for q in range(2):
                ps = psum.tile([P, J, 256], BF16, name="wk", tag="wk", bufs=3)
                for j in range(J):
                    c0 = h * HALF + q * 256
                    nc.tensor.matmul(
                        ps[:, j, :], lhsT=idb[:], rhs=s_t[b, k][:, j, c0 : c0 + 256], start=True, stop=True
                    )
                nc.scalar.copy(out=t[:, q * 256 : (q + 1) * 256, :], in_=ps[:].rearrange("p j n -> p n j"))

        def qs(b, k, h):
            quant(sq, b, k, h, "s", si[b, k, h], E4M3)

        def gt(b, k, gm):
            t = itile("t_int")
            ti[b, gm, k] = t
            words = g_t[b, k][:].bitcast(F32)
            dst = t[:].bitcast(F32).rearrange("p (i a c) u -> p i a c u", i=2, a=2)
            for i in range(2):
                ps = psum.tile([P, 2, 2, P], F32, name="wk", tag="wk", bufs=3)
                for a in range(2):
                    for u in range(2):
                        nc.tensor.transpose(
                            ps[:, a, u, :], words[:, 2 * i + a, gm * 256 + u : (gm + 1) * 256 : 2], idf[:]
                        )
                nc.scalar.copy(out=dst[:, i], in_=ps[:].rearrange("p a u c -> p a c u"))

        def qt(b, k, gm):
            quant(tq, b, gm, k, "t", ti[b, gm, k], E5M2)

        def td(b, k, h):
            t = itile("d_int")
            di[b, k, h] = t
            nc.scalar.copy(out=t[:], in_=dn_t[b, k][:, :, h * HALF : (h + 1) * HALF].rearrange("p j n -> p n j"))

        def qd(b, k, h):
            quant(dq, b, k, h, "d", di[b, k, h], E4M3)

        def mx(ps, left, right, cols, h, lf, rf, b):
            rc = slice(h * HALF, (h + 1) * HALF)
            for k in range(2):
                lc, ls = left[b, k]
                c, s = right[b, k]
                nc.tensor.matmul_mx(
                    ps[:],
                    lhsT=lc[:, cols].bitcast(lf),
                    lhsT_scale=ls[:, cols],
                    rhs=c[:, rc].bitcast(rf),
                    rhs_scale=s[:, rc],
                    start=(k == 0),
                    stop=(k == 1),
                )

        def o0(b, i):
            o = pout.tile([P, N], F32, name="o0", tag="o0", bufs=2)
            for h in range(2):
                ps = psum.tile([P, HALF], F32, name="wk", tag="wk", bufs=3)
                mx(ps, tq, dq, slice(i * P, (i + 1) * P), h, E5M2, E4M3, b)
                nc.scalar.copy(out=o[:, h * HALF : (h + 1) * HALF], in_=ps[:])
            nc.sync.dma_start(out=o0_v[b, i // J, i % J], in_=o[:])

        live = {}

        def e1(b, i):
            k, j = i // J, i % J
            mr = pout.tile([P, N], F32, name="mr", tag="mr", bufs=2)
            r = rinv[:, 2 * b + k, j : j + 1]
            nc.gpsimd.tensor_scalar(
                out=mr[:], in0=mask_t[b, k][:, j, :], scalar1=r, scalar2=1.0, op0=ALU.mult, op1=ALU.mult
            )
            acc = pout.tile([P, 2], F32, name="acc", tag="acc", bufs=3)
            banks = []
            for h in range(2):
                ps = psum.tile([P, HALF], F32, name="dd", tag="dd", bufs=5)
                mx(ps, gq, sq, slice(i * P, (i + 1) * P), h, E5M2, E4M3, b)
                banks.append(ps)
                junk = pout.tile([P, HALF], F32, name="junk", tag="junk", bufs=2)
                nc.vector.scalar_tensor_tensor(
                    out=junk[:],
                    in0=ps[:],
                    scalar=r,
                    in1=w_t[b, k][:, j, h * HALF : (h + 1) * HALF],
                    op0=ALU.mult,
                    op1=ALU.mult,
                    accum_out=acc[:, h : h + 1],
                )
            live[b, i] = (mr, acc, banks)

        def e2(b, i, e_next):
            k, j = i // J, i % J
            mr, acc, banks = live[b, i]
            c = pout.tile([P, 1], F32, name="c", tag="c", bufs=3)
            o = pout.tile([P, N], F32, name="o1", tag="o1", bufs=3)
            nc.vector.tensor_tensor(out=c[:], in0=acc[:, 0:1], in1=acc[:, 1:2], op=ALU.add)
            if e_next is not None:
                e1(*e_next)
            for h in range(2):
                cols = slice(h * HALF, (h + 1) * HALF)
                nc.vector.scalar_tensor_tensor(
                    out=o[:, cols],
                    in0=banks[h][:],
                    scalar=c[:],
                    in1=mr[:, cols],
                    op0=ALU.subtract,
                    op1=ALU.mult,
                )
            nc.sync.dma_start(out=o1_v[b, k, j], in_=o[:])

        wp(0, 0)
        gt(0, 0, 0)
        gt(0, 0, 1)
        tg(0, 0, 0, "v")
        tg(0, 0, 1, "v")
        qt(0, 0, 0)
        qt(0, 0, 1)
        qg(0, 0, 0)
        qg(0, 0, 1)
        tg(0, 1, 0, "s")
        tg(0, 1, 1, "v")
        gt(0, 1, 0)
        gt(0, 1, 1)
        load_g(1, 0)
        load_g(1, 1)
        sg(0, 0, 0)
        sg(0, 0, 1)
        qg(0, 1, 0)
        qg(0, 1, 1)
        wp(0, 1)
        sg(0, 1, 0)
        sg(0, 1, 1)
        load_s(1, 0)
        load_s(1, 1)
        for k in range(2):
            for h in range(2):
                qs(0, k, h)

        fill = {
            (0, 0): [(td, 0, 0, 0), (qt, 0, 1, 0), (qt, 0, 1, 1)],
            (0, 1): [(td, 0, 0, 1), (qd, 0, 0, 0)],
            (0, 2): [(td, 0, 1, 0), (qd, 0, 0, 1), (tg, 1, 0, 0, "s")],
            (0, 3): [(td, 0, 1, 1), (qd, 0, 1, 0), (load_w, 1, 1), (wp, 1, 0), (qg, 1, 0, 0)],
            (0, 4): [(qd, 0, 1, 1), (o0, 0, 0), (tg, 1, 0, 1, "s"), (o0, 0, 1), (qg, 1, 0, 1)],
            (0, 5): [(tg, 1, 1, 0, "s"), (o0, 0, 2), (tg, 1, 1, 1, "s"), (qg, 1, 1, 0)],
            (0, 6): [(sg, 1, 0, 0), (sg, 1, 0, 1), (qg, 1, 1, 1), (qs, 1, 0, 0), (o0, 0, 3), (wp, 1, 1)],
            (0, 7): [(sg, 1, 1, 0), (sg, 1, 1, 1), (qs, 1, 0, 1), (qs, 1, 1, 0), (qs, 1, 1, 1), (td, 1, 0, 0), (gt, 1, 0, 0)],
            (1, 0): [(td, 1, 0, 1), (qd, 1, 0, 0), (o0, 0, 4), (gt, 1, 0, 1), (qt, 1, 0, 0)],
            (1, 1): [(td, 1, 1, 0), (qd, 1, 0, 1), (gt, 1, 1, 0), (o0, 0, 5), (qt, 1, 0, 1)],
            (1, 2): [(td, 1, 1, 1), (gt, 1, 1, 1), (qd, 1, 1, 0), (qt, 1, 1, 0), (o0, 0, 6)],
            (1, 3): [(qd, 1, 1, 1), (qt, 1, 1, 1), (o0, 0, 7), (o0, 1, 0)],
            (1, 4): [(o0, 1, 1), (o0, 1, 2)],
            (1, 5): [(o0, 1, 3), (o0, 1, 4)],
            (1, 6): [(o0, 1, 5), (o0, 1, 6)],
            (1, 7): [(o0, 1, 7)],
        }
        blocks = [(b, i) for b in range(BS) for i in range(8)]
        e1(*blocks[0])
        for n, blk in enumerate(blocks):
            for f in fill[blk]:
                f[0](*f[1:])
            e2(*blk, blocks[n + 1] if n + 1 < len(blocks) else None)
